import numpy as np
import ml_dtypes

BF16 = ml_dtypes.bfloat16


def bf(x):
    return np.asarray(x, np.float32).astype(BF16)


def f32(x):
    return np.asarray(x, np.float32)


def f64(x):
    return np.asarray(x).astype(np.float64)


def striped(idx):
    return np.tile(idx.reshape(-1, 16).T, (8, 1))


V, E, F, H, D, N = 4096, 128, 512, 8, 128, 2048
M = H * D


def setup_inputs():
    return {
        "table": bf(np.random.standard_normal((E, V))),
        "ff_w": bf(np.random.standard_normal((E, F)) / np.sqrt(E)),
        "q_w": bf(np.random.standard_normal((F, M)) / np.sqrt(F)),
        "k_w": bf(np.random.standard_normal((F, M)) / np.sqrt(F)),
        "v_w": bf(np.random.standard_normal((F, M)) / np.sqrt(F)),
        "offs": striped(np.random.permutation(np.tile(np.arange(V), 2))[:N]),
    }


def reference(table, ff_w, q_w, k_w, v_w, offs):
    idx = offs[:16].T.reshape(-1)
    hf = np.maximum(f64(ff_w).T @ f64(table)[:, idx], 0.0)
    return np.concatenate([f64(q_w).T @ hf, f64(k_w).T @ hf, f64(v_w).T @ hf], axis=0)

@@ -1,0 +1,87 @@
+import concourse.mybir as mybir
+
+BF16, F32, U16 = mybir.dt.bfloat16, mybir.dt.float32, mybir.dt.uint16
+RELU = mybir.ActivationFunctionType.Relu
+
+P = 128
+V = 4096
+E = 128
+F = 512
+M = 1024
+N = 2048
+PIECE = 512
+N_PIECES = N // PIECE
+F_BLOCKS = F // P
+M_BLOCKS = M // P
+
+FLOPS = 2 * N * (E * F + F * 3 * M)
+
+
+def tile_modelconcept2_b_kernel(tc, table, ff_w, q_w, k_w, v_w, offs, out):
+    nc = tc.nc
+
+    with (
+        tc.tile_pool(name="held", bufs=1) as held,
+        tc.tile_pool(name="staging", bufs=6) as staging,
+        tc.psum_pool(name="psum", bufs=8) as psum,
+    ):
+        offsets = held.tile([P, N // 16], U16, name="offsets")
+        nc.sync.dma_start(offsets[:], offs)
+        ff_sb = held.tile([P, F], BF16, name="ff_sb")
+        nc.sync.dma_start(ff_sb[:], ff_w)
+        table_sb = held.tile([P, V], BF16, name="table_sb")
+        nc.sync.dma_start(table_sb[:], table)
+        proj_sb = []
+        for name, w in (("q_sb", q_w), ("k_sb", k_w), ("v_sb", v_w)):
+            w_sb = held.tile([P, F_BLOCKS, M], BF16, name=name)
+            nc.sync.dma_start(w_sb[:], w.rearrange("(b p) m -> p b m", p=P))
+            proj_sb.append(w_sb)
+
+        def empty_bank(turn, dst, bank, relu):
+            if turn % 2 == 0:
+                if relu:
+                    nc.vector.tensor_scalar_max(dst, bank, 0.0)
+                else:
+                    nc.vector.tensor_copy(dst, bank)
+            else:
+                if relu:
+                    nc.scalar.activation(dst, bank, RELU)
+                else:
+                    nc.scalar.copy(dst, bank)
+
+        hidden = [
+            [held.tile([P, PIECE], BF16, name=f"hidden_{j}_{b}") for b in range(F_BLOCKS)]
+            for j in range(N_PIECES)
+        ]
+        turn = 0
+        for j in range(N_PIECES):
+            piece_offsets = offsets[:, j * (PIECE // 16) : (j + 1) * (PIECE // 16)]
+            for b in range(F_BLOCKS):
+                acc = psum.tile([P, PIECE], F32, name="acc")
+                nc.tensor.matmul(
+                    acc[:],
+                    ff_sb[:, b * P : (b + 1) * P],
+                    table_sb[:].indirect(piece_offsets),
+                    start=True,
+                    stop=True,
+                )
+                empty_bank(turn, hidden[j][b][:], acc[:], relu=True)
+                turn += 1
+
+        for w_index, w_sb in enumerate(proj_sb):
+            for m in range(M_BLOCKS):
+                row0 = w_index * M + m * P
+                for j in range(N_PIECES):
+                    acc = psum.tile([P, PIECE], F32, name="acc")
+                    for b in range(F_BLOCKS):
+                        nc.tensor.matmul(
+                            acc[:],
+                            w_sb[:, b, m * P : (m + 1) * P],
+                            hidden[j][b][:],
+                            start=(b == 0),
+                            stop=(b == F_BLOCKS - 1),
+                        )
+                    staged = staging.tile([P, PIECE], F32, name="staged")
+                    empty_bank(turn, staged[:], acc[:], relu=False)
+                    turn += 1
+                    nc.sync.dma_start(out[row0 : row0 + P, j * PIECE : (j + 1) * PIECE], staged[:])

@@ -13,6 +13,7 @@ PIECE = 512
 N_PIECES = N // PIECE
 F_BLOCKS = F // P
 M_BLOCKS = M // P
+LAST_WIDTH = 128
 
 FLOPS = 2 * N * (E * F + F * 3 * M)
 
@@ -72,16 +73,20 @@ def tile_modelconcept2_b_kernel(tc, table, ff_w, q_w, k_w, v_w, offs, out):
             for m in range(M_BLOCKS):
                 row0 = w_index * M + m * P
                 for j in range(N_PIECES):
-                    acc = psum.tile([P, PIECE], F32, name="acc")
-                    for b in range(F_BLOCKS):
-                        nc.tensor.matmul(
-                            acc[:],
-                            w_sb[:, b, m * P : (m + 1) * P],
-                            hidden[j][b][:],
-                            start=(b == 0),
-                            stop=(b == F_BLOCKS - 1),
-                        )
-                    staged = staging.tile([P, PIECE], F32, name="staged")
-                    empty_bank(turn, staged[:], acc[:], relu=False)
-                    turn += 1
-                    nc.sync.dma_start(out[row0 : row0 + P, j * PIECE : (j + 1) * PIECE], staged[:])
+                    is_last_piece = row0 + P == 3 * M and j == N_PIECES - 1
+                    width = LAST_WIDTH if is_last_piece else PIECE
+                    for c in range(0, PIECE, width):
+                        acc = psum.tile([P, PIECE], F32, name="acc")
+                        for b in range(F_BLOCKS):
+                            nc.tensor.matmul(
+                                acc[:, :width],
+                                w_sb[:, b, m * P : (m + 1) * P],
+                                hidden[j][b][:, c : c + width],
+                                start=(b == 0),
+                                stop=(b == F_BLOCKS - 1),
+                            )
+                        staged = staging.tile([P, PIECE], F32, name="staged")
+                        empty_bank(turn, staged[:, :width], acc[:, :width], relu=False)
+                        turn += 1
+                        col0 = j * PIECE + c
+                        nc.sync.dma_start(out[row0 : row0 + P, col0 : col0 + width], staged[:, :width])

@@ -13,7 +13,7 @@ PIECE = 512
 N_PIECES = N // PIECE
 F_BLOCKS = F // P
 M_BLOCKS = M // P
-LAST_WIDTH = 128
+LAST_WIDTH = 256
 
 FLOPS = 2 * N * (E * F + F * 3 * M)
 

import concourse.mybir as mybir

BF16, F32, U16 = mybir.dt.bfloat16, mybir.dt.float32, mybir.dt.uint16
RELU = mybir.ActivationFunctionType.Relu

P = 128
V = 4096
E = 128
F = 512
M = 1024
N = 2048
PIECE = 512
N_PIECES = N // PIECE
F_BLOCKS = F // P
M_BLOCKS = M // P
LAST_WIDTH = 256

FLOPS = 2 * N * (E * F + F * 3 * M)


def tile_modelconcept2_b_kernel(tc, table, ff_w, q_w, k_w, v_w, offs, out):
    nc = tc.nc

    with (
        tc.tile_pool(name="held", bufs=1) as held,
        tc.tile_pool(name="staging", bufs=6) as staging,
        tc.psum_pool(name="psum", bufs=8) as psum,
    ):
        offsets = held.tile([P, N // 16], U16, name="offsets")
        nc.sync.dma_start(offsets[:], offs)
        ff_sb = held.tile([P, F], BF16, name="ff_sb")
        nc.sync.dma_start(ff_sb[:], ff_w)
        table_sb = held.tile([P, V], BF16, name="table_sb")
        nc.sync.dma_start(table_sb[:], table)
        proj_sb = []
        for name, w in (("q_sb", q_w), ("k_sb", k_w), ("v_sb", v_w)):
            w_sb = held.tile([P, F_BLOCKS, M], BF16, name=name)
            nc.sync.dma_start(w_sb[:], w.rearrange("(b p) m -> p b m", p=P))
            proj_sb.append(w_sb)

        def empty_bank(turn, dst, bank, relu):
            if turn % 2 == 0:
                if relu:
                    nc.vector.tensor_scalar_max(dst, bank, 0.0)
                else:
                    nc.vector.tensor_copy(dst, bank)
            else:
                if relu:
                    nc.scalar.activation(dst, bank, RELU)
                else:
                    nc.scalar.copy(dst, bank)

        hidden = [
            [held.tile([P, PIECE], BF16, name=f"hidden_{j}_{b}") for b in range(F_BLOCKS)]
            for j in range(N_PIECES)
        ]
        turn = 0
        for j in range(N_PIECES):
            piece_offsets = offsets[:, j * (PIECE // 16) : (j + 1) * (PIECE // 16)]
            for b in range(F_BLOCKS):
                acc = psum.tile([P, PIECE], F32, name="acc")
                nc.tensor.matmul(
                    acc[:],
                    ff_sb[:, b * P : (b + 1) * P],
                    table_sb[:].indirect(piece_offsets),
                    start=True,
                    stop=True,
                )
                empty_bank(turn, hidden[j][b][:], acc[:], relu=True)
                turn += 1

        for w_index, w_sb in enumerate(proj_sb):
            for m in range(M_BLOCKS):
                row0 = w_index * M + m * P
                for j in range(N_PIECES):
                    is_last_piece = row0 + P == 3 * M and j == N_PIECES - 1
                    width = LAST_WIDTH if is_last_piece else PIECE
                    for c in range(0, PIECE, width):
                        acc = psum.tile([P, PIECE], F32, name="acc")
                        for b in range(F_BLOCKS):
                            nc.tensor.matmul(
                                acc[:, :width],
                                w_sb[:, b, m * P : (m + 1) * P],
                                hidden[j][b][:, c : c + width],
                                start=(b == 0),
                                stop=(b == F_BLOCKS - 1),
                            )
                        staged = staging.tile([P, PIECE], F32, name="staged")
                        empty_bank(turn, staged[:, :width], acc[:, :width], relu=False)
                        turn += 1
                        col0 = j * PIECE + c
                        nc.sync.dma_start(out[row0 : row0 + P, col0 : col0 + width], staged[:, :width])
